import numpy as np
import ml_dtypes


def mxq(x, axis, fmt="e4m3"):
    dtype, down = {"e4m3": (ml_dtypes.float8_e4m3fn, 7), "e5m2": (ml_dtypes.float8_e5m2, 14)}[fmt]
    v = np.moveaxis(np.asarray(x, np.float32).astype(ml_dtypes.bfloat16).astype(np.float64), axis, -1)
    blocks = v.reshape(v.shape[:-1] + (-1, 32))
    amax = np.abs(blocks).max(-1, keepdims=True)
    byte = np.maximum(np.where(amax > 0, np.frexp(amax)[1] - 1 + 127, 0) - down, 1)
    scale = np.exp2(byte - 127.0)
    codes = (blocks / scale).astype(np.float32).astype(dtype).astype(np.float64)
    return np.moveaxis((codes * scale).reshape(v.shape), -1, axis)


WIDE = False


def mx_kscale(k):
    if not WIDE:
        return np.ones(k)
    levels = np.array([10, -10, 5, -5, 0])
    a = np.random.permutation(np.resize(levels, k // 512 * 4)).reshape(k // 512, 4)
    idx = np.arange(k)
    return np.exp2(a[idx // 512, idx % 128 // 32])


BF16 = ml_dtypes.bfloat16


def bf(x):
    return np.asarray(x, np.float32).astype(BF16)


def f64(x):
    return np.asarray(x).astype(np.float64)


E2M1 = np.array([0.0, 0.5, 1.0, 1.5, 2.0, 3.0, 4.0, 6.0, -0.0, -0.5, -1.0, -1.5, -2.0, -3.0, -4.0, -6.0])


def pack_weight(w, fmt):
    k, n = w.shape
    w = f64(bf(w)).reshape(k // 32, 32, n)
    amax = np.abs(w).max(1)
    if fmt == "e4m3":
        byte = np.frexp(amax)[1] - 1 + 127 - 7
    else:
        mant, ex = np.frexp(amax / 6.0)
        byte = np.where(mant > 0.5, ex, ex - 1) + 127
    byte = np.clip(np.where(amax > 0, byte, 1), 1, 254)
    scaled = (w * np.exp2(127.0 - byte)[:, None, :]).reshape(k, n).astype(np.float32)
    by_word = np.ascontiguousarray(scaled.reshape(k // 512, 128, 4, n).transpose(0, 1, 3, 2))
    if fmt == "e4m3":
        words = by_word.astype(ml_dtypes.float8_e4m3fn).view(np.uint8)
    else:
        c = by_word.astype(ml_dtypes.float4_e2m1fn).view(np.uint8) & 0xF
        words = c[..., 0::2] | (c[..., 1::2] << 4)
    return np.ascontiguousarray(words), np.ascontiguousarray(byte.astype(np.uint8).reshape(k // 512, 16, n))


def unpack_weight(words, scales, fmt):
    g, p, n, _ = words.shape
    if fmt == "e4m3":
        vals = np.ascontiguousarray(words).view(ml_dtypes.float8_e4m3fn).astype(np.float64)
    else:
        nib = np.empty((g, p, n, 4), np.uint8)
        nib[..., 0::2] = words & 0xF
        nib[..., 1::2] = words >> 4
        vals = E2M1[nib]
    vals = vals * np.repeat(np.exp2(scales.astype(np.float64) - 127.0), 8, axis=1)[..., None]
    return vals.transpose(0, 1, 3, 2).reshape(g * 512, n)


N, E, C, D1, D2 = 16384, 512, 128, 2, 2
T1 = D1 + 1


def shift_down(y, k):
    return np.pad(y, ((k, 0), (0, 0)))[:y.shape[0]] if k > 0 else y


def setup_inputs():
    s = mx_kscale(E)
    x = bf(np.random.standard_normal((N, E)) * s)
    W1 = np.random.standard_normal((T1, E, C)) * 0.4 / np.sqrt(E) / s[None, :, None]
    W1_words, W1_scales = pack_weight(W1.reshape(-1, C), "e4m3")
    b1 = bf(np.random.standard_normal((1, C)) * 0.25)
    return {"x": x, "W1_words": W1_words, "W1_scales": W1_scales, "b1": b1}


def reference(x, W1_words, W1_scales, b1):
    Y = mxq(f64(x), 1, "e4m3") @ unpack_weight(W1_words, W1_scales, "e4m3").reshape(T1, E, C)
    S = sum(shift_down(Y[k], k) for k in range(T1))
    cnt1 = np.minimum(np.arange(N), D1) + 1.0
    return np.tanh(S + cnt1[:, None] * f64(b1)[0])

@@ -1,0 +1,172 @@
+from contextlib import ExitStack
+
+import concourse.mybir as mybir
+from concourse.masks import make_identity
+
+F32 = mybir.dt.float32
+BF16 = mybir.dt.bfloat16
+I32 = mybir.dt.int32
+U32 = mybir.dt.uint32
+U8 = mybir.dt.uint8
+FP8X4 = mybir.dt.float8_e4m3fn_x4
+
+P = 128
+ROWS = 16384
+K = 512
+C = 128
+TAPS = 3
+HALO = TAPS - 1
+SECTIONS = ROWS // P
+WORDS = K // 2
+PAIRS = 2
+
+ROUND = 8
+ROUNDS = SECTIONS // ROUND
+XT_SECTIONS = 2
+ACC_SECTIONS = 4
+PREFETCH = 4
+
+FLOPS = 2 * ROWS * TAPS * K * C
+
+
+def tile_predictor_pa_t_e_kernel(tc, x, W1_words, W1_scales, b1, out):
+    nc = tc.nc
+    x_sections = x.rearrange("(j t) k -> j t k", t=SECTIONS)
+    out_sections = out.rearrange("(j t) c -> j t c", t=SECTIONS)
+
+    with ExitStack() as ctx:
+        const = ctx.enter_context(tc.tile_pool(name="const", bufs=1))
+        x_pool = ctx.enter_context(tc.tile_pool(name="x_pool", bufs=PREFETCH + 2))
+        grouped_pool = ctx.enter_context(tc.tile_pool(name="grouped_pool", bufs=3))
+        result_pool = ctx.enter_context(tc.tile_pool(name="result_pool", bufs=3))
+        xt_pool = ctx.enter_context(tc.psum_pool(name="xt_pool", bufs=4))
+        acc_pool = ctx.enter_context(tc.psum_pool(name="acc_pool", bufs=4))
+        ctx.enter_context(tc.manual_schedule())
+
+        x_codes = const.tile([P, HALO + SECTIONS, P], U32, align_bytes=64)
+        x_scales = const.tile([P, HALO + SECTIONS, P], U8, align_bytes=64)
+
+        def load_sections(x_tile, first, count):
+            nc.sync.dma_start(out=x_tile[:], in_=x_sections[:, first : first + count, :])
+
+        def transpose_sections(x_tile, grouped, count, shift):
+            words_in = x_tile[:].bitcast(F32)
+            words_out = grouped[:].bitcast(F32)
+            for bank in range(count // XT_SECTIONS):
+                first = bank * XT_SECTIONS
+                xt = xt_pool.tile([P, XT_SECTIONS, PAIRS, P], F32, name="xt")
+                for s in range(XT_SECTIONS):
+                    for u in range(PAIRS):
+                        nc.tensor.transpose(
+                            xt[:, s, u, :], words_in[:, first + s, u:WORDS:PAIRS], identity[:]
+                        )
+                copy = nc.vector.tensor_copy if bank % 4 == 3 else nc.scalar.copy
+                copy(
+                    out=words_out[:, first : first + XT_SECTIONS, shift:P, :],
+                    in_=xt[:].rearrange("p s u j -> p s j u")[:, :, 0 : P - shift, :],
+                )
+
+        def quantise_sections(grouped, position, count):
+            nc.vector.quantize_mx(
+                out=x_codes[:, position : position + count, :]
+                .rearrange("p s j -> p (s j)")
+                .bitcast(FP8X4),
+                scales=x_scales[:, position : position + count, :].rearrange("p s j -> p (s j)"),
+                in_=grouped[:].rearrange("p s j t -> p (s j t)"),
+            )
+
+        def multiply_round(r, result):
+            for half in range(ROUND // ACC_SECTIONS):
+                first = r * ROUND + half * ACC_SECTIONS
+                acc = acc_pool.tile([P, ACC_SECTIONS, C], F32, name="acc")
+                for q in range(ACC_SECTIONS):
+                    for tap in range(TAPS):
+                        position = HALO + first + q - tap
+                        nc.tensor.matmul_mx(
+                            out=acc[:, q, :],
+                            lhsT=x_codes[:, position, :].bitcast(FP8X4),
+                            lhsT_scale=x_scales[:, position, :],
+                            rhs=w_codes[:, tap, :].bitcast(FP8X4),
+                            rhs_scale=w_scales[:, tap, :],
+                            start=(tap == 0),
+                            stop=(tap == TAPS - 1),
+                        )
+                bias = bias_head if first == 0 else bias_full
+                nc.vector.tensor_tensor(
+                    out=result[:, half * ACC_SECTIONS : (half + 1) * ACC_SECTIONS, :],
+                    in0=acc[:],
+                    in1=bias[:],
+                    op=mybir.AluOpType.add,
+                )
+
+        def finish_round(r, result):
+            nc.scalar.activation(
+                out=result[:], in_=result[:], func=mybir.ActivationFunctionType.Tanh
+            )
+            nc.sync.dma_start(out=out_sections[:, r * ROUND : (r + 1) * ROUND, :], in_=result[:])
+
+        x_halo = const.tile([P, HALO, K], BF16)
+        load_sections(x_halo, SECTIONS - HALO, HALO)
+        x_tiles = {}
+        x_tiles[0] = x_pool.tile([P, ROUND, K], BF16, name="x_tile")
+        load_sections(x_tiles[0], 0, ROUND)
+
+        w_codes = const.tile([P, TAPS, 4 * C], U8, align_bytes=64)
+        nc.sync.dma_start(
+            out=w_codes[:].bitcast(I32),
+            in_=W1_words.rearrange("g p n t -> p g (n t)").bitcast(I32),
+        )
+        w_scales = const.tile([P, TAPS, C], U8, align_bytes=64)
+        nc.vector.memset(w_scales[:].bitcast(I32), 0)
+        scale_rows = W1_scales.bitcast(I32).rearrange("g q n -> q g n")
+        for quadrant in range(4):
+            nc.sync.dma_start(
+                out=w_scales[32 * quadrant : 32 * quadrant + 4, :, :].bitcast(I32),
+                in_=scale_rows[4 * quadrant : 4 * quadrant + 4, :, :],
+            )
+        for r in range(1, PREFETCH):
+            x_tiles[r] = x_pool.tile([P, ROUND, K], BF16, name="x_tile")
+            load_sections(x_tiles[r], r * ROUND, ROUND)
+
+        b1_rows = const.tile([P, C], BF16)
+        nc.scalar.dma_start(out=b1_rows[:], in_=b1[0].partition_broadcast(P))
+
+        identity = const.tile([P, P], F32)
+        make_identity(nc, identity[:])
+        warm = const.tile([P, 1], F32)
+        nc.vector.memset(warm[:], 0.0)
+        nc.scalar.activation(out=warm[:], in_=warm[:], func=mybir.ActivationFunctionType.Tanh)
+
+        grouped_halo = const.tile([P, HALO, P, 4], BF16, align_bytes=64)
+        nc.vector.memset(grouped_halo[:], 0.0)
+        transpose_sections(x_halo, grouped_halo, HALO, 1)
+        quantise_sections(grouped_halo, 0, HALO)
+
+        bias_full = const.tile([P, ACC_SECTIONS, C], F32)
+        bias_head = const.tile([P, ACC_SECTIONS, C], F32)
+        for q in range(ACC_SECTIONS):
+            nc.vector.tensor_scalar_mul(out=bias_full[:, q, :], in0=b1_rows[:], scalar1=float(TAPS))
+            nc.vector.tensor_scalar_mul(out=bias_head[:, q, :], in0=b1_rows[:], scalar1=float(TAPS))
+        for q in range(HALO):
+            nc.vector.tensor_scalar_mul(
+                out=bias_head[0:1, q, :], in0=b1_rows[0:1, :], scalar1=float(q + 1)
+            )
+
+        grouped_tiles = {}
+        result_tiles = {}
+        for i in range(ROUNDS + 3):
+            if i + PREFETCH < ROUNDS:
+                x_tiles[i + PREFETCH] = x_pool.tile([P, ROUND, K], BF16, name="x_tile")
+                load_sections(x_tiles[i + PREFETCH], (i + PREFETCH) * ROUND, ROUND)
+            if 0 <= i - 1 < ROUNDS:
+                quantise_sections(grouped_tiles[i - 1], HALO + (i - 1) * ROUND, ROUND)
+            if i < ROUNDS:
+                grouped_tiles[i] = grouped_pool.tile(
+                    [P, ROUND, P, 4], BF16, name="grouped", align_bytes=64
+                )
+                transpose_sections(x_tiles[i], grouped_tiles[i], ROUND, 0)
+            if 0 <= i - 2 < ROUNDS:
+                result_tiles[i - 2] = result_pool.tile([P, ROUND, C], F32, name="result")
+                multiply_round(i - 2, result_tiles[i - 2])
+            if 0 <= i - 3:
+                finish_round(i - 3, result_tiles[i - 3])

@@ -17,14 +17,14 @@ C = 128
 TAPS = 3
 HALO = TAPS - 1
 SECTIONS = ROWS // P
-WORDS = K // 2
 PAIRS = 2
 
 ROUND = 8
 ROUNDS = SECTIONS // ROUND
 XT_SECTIONS = 2
 ACC_SECTIONS = 4
-PREFETCH = 4
+LOAD_AHEAD = 6
+SORT_AHEAD = 2
 
 FLOPS = 2 * ROWS * TAPS * K * C
 
@@ -36,7 +36,8 @@ def tile_predictor_pa_t_e_kernel(tc, x, W1_words, W1_scales, b1, out):
 
     with ExitStack() as ctx:
         const = ctx.enter_context(tc.tile_pool(name="const", bufs=1))
-        x_pool = ctx.enter_context(tc.tile_pool(name="x_pool", bufs=PREFETCH + 2))
+        x_pool = ctx.enter_context(tc.tile_pool(name="x_pool", bufs=LOAD_AHEAD))
+        sorted_pool = ctx.enter_context(tc.tile_pool(name="sorted_pool", bufs=4))
         grouped_pool = ctx.enter_context(tc.tile_pool(name="grouped_pool", bufs=3))
         result_pool = ctx.enter_context(tc.tile_pool(name="result_pool", bufs=3))
         xt_pool = ctx.enter_context(tc.psum_pool(name="xt_pool", bufs=4))
@@ -49,19 +50,21 @@ def tile_predictor_pa_t_e_kernel(tc, x, W1_words, W1_scales, b1, out):
         def load_sections(x_tile, first, count):
             nc.sync.dma_start(out=x_tile[:], in_=x_sections[:, first : first + count, :])
 
-        def transpose_sections(x_tile, grouped, count, shift):
-            words_in = x_tile[:].bitcast(F32)
+        def sort_sections(x_tile, x_sorted):
+            nc.vector.tensor_copy(
+                out=x_sorted[:],
+                in_=x_tile[:].bitcast(F32).rearrange("j s (p u) -> j s u p", u=PAIRS),
+            )
+
+        def transpose_sections(x_sorted, grouped, count, shift):
             words_out = grouped[:].bitcast(F32)
             for bank in range(count // XT_SECTIONS):
                 first = bank * XT_SECTIONS
                 xt = xt_pool.tile([P, XT_SECTIONS, PAIRS, P], F32, name="xt")
                 for s in range(XT_SECTIONS):
                     for u in range(PAIRS):
-                        nc.tensor.transpose(
-                            xt[:, s, u, :], words_in[:, first + s, u:WORDS:PAIRS], identity[:]
-                        )
-                copy = nc.vector.tensor_copy if bank % 4 == 3 else nc.scalar.copy
-                copy(
+                        nc.tensor.transpose(xt[:, s, u, :], x_sorted[:, first + s, u, :], identity[:])
+                nc.scalar.copy(
                     out=words_out[:, first : first + XT_SECTIONS, shift:P, :],
                     in_=xt[:].rearrange("p s u j -> p s j u")[:, :, 0 : P - shift, :],
                 )
@@ -75,10 +78,12 @@ def tile_predictor_pa_t_e_kernel(tc, x, W1_words, W1_scales, b1, out):
                 in_=grouped[:].rearrange("p s j t -> p (s j t)"),
             )
 
-        def multiply_round(r, result):
+        def multiply_round(r):
+            banks = []
             for half in range(ROUND // ACC_SECTIONS):
                 first = r * ROUND + half * ACC_SECTIONS
                 acc = acc_pool.tile([P, ACC_SECTIONS, C], F32, name="acc")
+                banks.append(acc)
                 for q in range(ACC_SECTIONS):
                     for tap in range(TAPS):
                         position = HALO + first + q - tap
@@ -91,15 +96,21 @@ def tile_predictor_pa_t_e_kernel(tc, x, W1_words, W1_scales, b1, out):
                             start=(tap == 0),
                             stop=(tap == TAPS - 1),
                         )
-                bias = bias_head if first == 0 else bias_full
+            return banks
+
+        def add_bias(r, banks):
+            result = result_pool.tile([P, ROUND, C], F32, name="result")
+            for half in range(ROUND // ACC_SECTIONS):
+                bias = bias_head if r == 0 and half == 0 else bias_full
                 nc.vector.tensor_tensor(
                     out=result[:, half * ACC_SECTIONS : (half + 1) * ACC_SECTIONS, :],
-                    in0=acc[:],
+                    in0=banks[half][:],
                     in1=bias[:],
                     op=mybir.AluOpType.add,
                 )
+            return result
 
-        def finish_round(r, result):
+        def tanh_and_store(r, result):
             nc.scalar.activation(
                 out=result[:], in_=result[:], func=mybir.ActivationFunctionType.Tanh
             )
@@ -124,7 +135,7 @@ def tile_predictor_pa_t_e_kernel(tc, x, W1_words, W1_scales, b1, out):
                 out=w_scales[32 * quadrant : 32 * quadrant + 4, :, :].bitcast(I32),
                 in_=scale_rows[4 * quadrant : 4 * quadrant + 4, :, :],
             )
-        for r in range(1, PREFETCH):
+        for r in range(1, LOAD_AHEAD):
             x_tiles[r] = x_pool.tile([P, ROUND, K], BF16, name="x_tile")
             load_sections(x_tiles[r], r * ROUND, ROUND)
 
@@ -139,7 +150,13 @@ def tile_predictor_pa_t_e_kernel(tc, x, W1_words, W1_scales, b1, out):
 
         grouped_halo = const.tile([P, HALO, P, 4], BF16, align_bytes=64)
         nc.vector.memset(grouped_halo[:], 0.0)
-        transpose_sections(x_halo, grouped_halo, HALO, 1)
+        halo_sorted = const.tile([P, HALO, PAIRS, P], F32)
+        sort_sections(x_halo, halo_sorted)
+        transpose_sections(halo_sorted, grouped_halo, HALO, 1)
+        sorted_tiles = {}
+        for r in range(SORT_AHEAD):
+            sorted_tiles[r] = sorted_pool.tile([P, ROUND, PAIRS, P], F32, name="x_sorted")
+            sort_sections(x_tiles[r], sorted_tiles[r])
         quantise_sections(grouped_halo, 0, HALO)
 
         bias_full = const.tile([P, ACC_SECTIONS, C], F32)
@@ -153,20 +170,27 @@ def tile_predictor_pa_t_e_kernel(tc, x, W1_words, W1_scales, b1, out):
             )
 
         grouped_tiles = {}
+        acc_banks = {}
         result_tiles = {}
         for i in range(ROUNDS + 3):
-            if i + PREFETCH < ROUNDS:
-                x_tiles[i + PREFETCH] = x_pool.tile([P, ROUND, K], BF16, name="x_tile")
-                load_sections(x_tiles[i + PREFETCH], (i + PREFETCH) * ROUND, ROUND)
+            if i + LOAD_AHEAD < ROUNDS:
+                x_tiles[i + LOAD_AHEAD] = x_pool.tile([P, ROUND, K], BF16, name="x_tile")
+                load_sections(x_tiles[i + LOAD_AHEAD], (i + LOAD_AHEAD) * ROUND, ROUND)
+            if 0 <= i - 3:
+                result_tiles[i - 3] = add_bias(i - 3, acc_banks[i - 3])
             if 0 <= i - 1 < ROUNDS:
                 quantise_sections(grouped_tiles[i - 1], HALO + (i - 1) * ROUND, ROUND)
+            if i + SORT_AHEAD < ROUNDS:
+                sorted_tiles[i + SORT_AHEAD] = sorted_pool.tile(
+                    [P, ROUND, PAIRS, P], F32, name="x_sorted"
+                )
+                sort_sections(x_tiles[i + SORT_AHEAD], sorted_tiles[i + SORT_AHEAD])
             if i < ROUNDS:
                 grouped_tiles[i] = grouped_pool.tile(
                     [P, ROUND, P, 4], BF16, name="grouped", align_bytes=64
                 )
-                transpose_sections(x_tiles[i], grouped_tiles[i], ROUND, 0)
+                transpose_sections(sorted_tiles[i], grouped_tiles[i], ROUND, 0)
             if 0 <= i - 2 < ROUNDS:
-                result_tiles[i - 2] = result_pool.tile([P, ROUND, C], F32, name="result")
-                multiply_round(i - 2, result_tiles[i - 2])
+                acc_banks[i - 2] = multiply_round(i - 2)
             if 0 <= i - 3:
-                finish_round(i - 3, result_tiles[i - 3])
+                tanh_and_store(i - 3, result_tiles[i - 3])

@@ -19,12 +19,12 @@ HALO = TAPS - 1
 SECTIONS = ROWS // P
 PAIRS = 2
 
-ROUND = 8
-ROUNDS = SECTIONS // ROUND
+CHUNKS = (2,2,4,8,8,8,8,8,8,8,8,8,8,8,8,8,8,4,2,2)
 XT_SECTIONS = 2
 ACC_SECTIONS = 4
-LOAD_AHEAD = 6
+LOAD_AHEAD = 7
 SORT_AHEAD = 2
+QUANTISE_WIDTHS = (8, 4, 2)
 
 FLOPS = 2 * ROWS * TAPS * K * C
 
@@ -33,64 +33,98 @@ def tile_predictor_pa_t_e_kernel(tc, x, W1_words, W1_scales, b1, out):
     nc = tc.nc
     x_sections = x.rearrange("(j t) k -> j t k", t=SECTIONS)
     out_sections = out.rearrange("(j t) c -> j t c", t=SECTIONS)
+    n_chunks = len(CHUNKS)
+    assert sum(CHUNKS) == SECTIONS and CHUNKS[0] == HALO
+    firsts = [(sum(CHUNKS[:c]) - HALO) % SECTIONS for c in range(n_chunks)]
+    outputs = [list(range(firsts[c], firsts[c] + CHUNKS[c])) for c in range(n_chunks)]
+    outputs[n_chunks - 1].extend(outputs[0])
+    outputs[0] = []
+    most_outputs = max(len(o) for o in outputs)
+    most_sections = max(CHUNKS)
 
     with ExitStack() as ctx:
         const = ctx.enter_context(tc.tile_pool(name="const", bufs=1))
-        x_pool = ctx.enter_context(tc.tile_pool(name="x_pool", bufs=LOAD_AHEAD))
+        x_pool = ctx.enter_context(tc.tile_pool(name="x_pool", bufs=7))
         sorted_pool = ctx.enter_context(tc.tile_pool(name="sorted_pool", bufs=4))
         grouped_pool = ctx.enter_context(tc.tile_pool(name="grouped_pool", bufs=3))
-        result_pool = ctx.enter_context(tc.tile_pool(name="result_pool", bufs=3))
+        result_pool = ctx.enter_context(tc.tile_pool(name="result_pool", bufs=6))
         xt_pool = ctx.enter_context(tc.psum_pool(name="xt_pool", bufs=4))
         acc_pool = ctx.enter_context(tc.psum_pool(name="acc_pool", bufs=4))
         ctx.enter_context(tc.manual_schedule())
 
-        x_codes = const.tile([P, HALO + SECTIONS, P], U32, align_bytes=64)
-        x_scales = const.tile([P, HALO + SECTIONS, P], U8, align_bytes=64)
+        x_codes = const.tile([P, SECTIONS, P], U32, align_bytes=64)
+        x_scales = const.tile([P, SECTIONS, P], U8, align_bytes=64)
+        halo_codes = const.tile([P, HALO, P], U32, align_bytes=64)
+        halo_scales = const.tile([P, HALO, P], U8, align_bytes=64)
 
-        def load_sections(x_tile, first, count):
-            nc.sync.dma_start(out=x_tile[:], in_=x_sections[:, first : first + count, :])
-
-        def sort_sections(x_tile, x_sorted):
-            nc.vector.tensor_copy(
-                out=x_sorted[:],
-                in_=x_tile[:].bitcast(F32).rearrange("j s (p u) -> j s u p", u=PAIRS),
+        def load_chunk(c):
+            x_tile = x_pool.tile([P, most_sections, K], BF16, name="x_tile")
+            nc.sync.dma_start(
+                out=x_tile[:, 0 : CHUNKS[c], :], in_=x_sections[:, firsts[c] : firsts[c] + CHUNKS[c], :]
             )
+            return x_tile
 
-        def transpose_sections(x_sorted, grouped, count, shift):
+        def sort_chunk(c, x_tile):
+            x_sorted = sorted_pool.tile([P, most_sections, PAIRS, P], F32, name="x_sorted")
+            nc.vector.tensor_copy(
+                out=x_sorted[:, 0 : CHUNKS[c], :, :],
+                in_=x_tile[:, 0 : CHUNKS[c], :].bitcast(F32).rearrange("j s (p u) -> j s u p", u=PAIRS),
+            )
+            return x_sorted
+
+        def transpose_chunk(c, x_sorted):
+            grouped = grouped_pool.tile([P, most_sections, P, 4], BF16, name="grouped", align_bytes=64)
             words_out = grouped[:].bitcast(F32)
-            for bank in range(count // XT_SECTIONS):
-                first = bank * XT_SECTIONS
+            for first in range(0, CHUNKS[c], XT_SECTIONS):
                 xt = xt_pool.tile([P, XT_SECTIONS, PAIRS, P], F32, name="xt")
                 for s in range(XT_SECTIONS):
                     for u in range(PAIRS):
                         nc.tensor.transpose(xt[:, s, u, :], x_sorted[:, first + s, u, :], identity[:])
                 nc.scalar.copy(
-                    out=words_out[:, first : first + XT_SECTIONS, shift:P, :],
-                    in_=xt[:].rearrange("p s u j -> p s j u")[:, :, 0 : P - shift, :],
+                    out=words_out[:, first : first + XT_SECTIONS, :, :],
+                    in_=xt[:].rearrange("p s u j -> p s j u"),
                 )
+            return grouped
 
-        def quantise_sections(grouped, position, count):
-            nc.vector.quantize_mx(
-                out=x_codes[:, position : position + count, :]
-                .rearrange("p s j -> p (s j)")
-                .bitcast(FP8X4),
-                scales=x_scales[:, position : position + count, :].rearrange("p s j -> p (s j)"),
-                in_=grouped[:].rearrange("p s j t -> p (s j t)"),
+        def quantise_chunk(c, grouped):
+            done = 0
+            while done < CHUNKS[c]:
+                count = max(w for w in QUANTISE_WIDTHS if w <= CHUNKS[c] - done)
+                t = firsts[c] + done
+                nc.vector.quantize_mx(
+                    out=x_codes[:, t : t + count, :].rearrange("p s j -> p (s j)").bitcast(FP8X4),
+                    scales=x_scales[:, t : t + count, :].rearrange("p s j -> p (s j)"),
+                    in_=grouped[:, done : done + count, :, :].rearrange("p s j t -> p (s j t)"),
+                )
+                done += count
+
+        def make_halo():
+            nc.vector.tensor_copy(
+                out=halo_codes[:, :, 1:P].bitcast(I32),
+                in_=x_codes[:, SECTIONS - HALO : SECTIONS, 0 : P - 1].bitcast(I32),
+            )
+            nc.vector.tensor_copy(
+                out=halo_scales[:, :, 1:P], in_=x_scales[:, SECTIONS - HALO : SECTIONS, 0 : P - 1]
             )
 
-        def multiply_round(r):
+        def stationary(t):
+            if t < 0:
+                return halo_codes[:, HALO + t, :], halo_scales[:, HALO + t, :]
+            return x_codes[:, t, :], x_scales[:, t, :]
+
+        def multiply_chunk(c):
             banks = []
-            for half in range(ROUND // ACC_SECTIONS):
-                first = r * ROUND + half * ACC_SECTIONS
+            for g in range(0, len(outputs[c]), ACC_SECTIONS):
+                group = outputs[c][g : g + ACC_SECTIONS]
                 acc = acc_pool.tile([P, ACC_SECTIONS, C], F32, name="acc")
-                banks.append(acc)
-                for q in range(ACC_SECTIONS):
+                banks.append((acc, group))
+                for q in range(len(group)):
                     for tap in range(TAPS):
-                        position = HALO + first + q - tap
+                        codes, scales = stationary(group[q] - tap)
                         nc.tensor.matmul_mx(
                             out=acc[:, q, :],
-                            lhsT=x_codes[:, position, :].bitcast(FP8X4),
-                            lhsT_scale=x_scales[:, position, :],
+                            lhsT=codes.bitcast(FP8X4),
+                            lhsT_scale=scales,
                             rhs=w_codes[:, tap, :].bitcast(FP8X4),
                             rhs_scale=w_scales[:, tap, :],
                             start=(tap == 0),
@@ -98,30 +132,37 @@ def tile_predictor_pa_t_e_kernel(tc, x, W1_words, W1_scales, b1, out):
                         )
             return banks
 
-        def add_bias(r, banks):
-            result = result_pool.tile([P, ROUND, C], F32, name="result")
-            for half in range(ROUND // ACC_SECTIONS):
-                bias = bias_head if r == 0 and half == 0 else bias_full
+        def add_bias(banks):
+            result = result_pool.tile([P, most_outputs, C], F32, name="result")
+            at = 0
+            for acc, group in banks:
+                bias = bias_head if 0 in group else bias_full
                 nc.vector.tensor_tensor(
-                    out=result[:, half * ACC_SECTIONS : (half + 1) * ACC_SECTIONS, :],
-                    in0=banks[half][:],
-                    in1=bias[:],
+                    out=result[:, at : at + len(group), :],
+                    in0=acc[:, 0 : len(group), :],
+                    in1=bias[:, 0 : len(group), :],
                     op=mybir.AluOpType.add,
                 )
+                at += len(group)
             return result
 
-        def tanh_and_store(r, result):
+        def tanh_and_store(c, result):
+            count = len(outputs[c])
             nc.scalar.activation(
-                out=result[:], in_=result[:], func=mybir.ActivationFunctionType.Tanh
+                out=result[:, 0:count, :], in_=result[:, 0:count, :], func=mybir.ActivationFunctionType.Tanh
             )
-            nc.sync.dma_start(out=out_sections[:, r * ROUND : (r + 1) * ROUND, :], in_=result[:])
+            at = 0
+            while at < count:
+                run = 1
+                while at + run < count and outputs[c][at + run] == outputs[c][at] + run:
+                    run += 1
+                t = outputs[c][at]
+                nc.sync.dma_start(out=out_sections[:, t : t + run, :], in_=result[:, at : at + run, :])
+                at += run
 
-        x_halo = const.tile([P, HALO, K], BF16)
-        load_sections(x_halo, SECTIONS - HALO, HALO)
         x_tiles = {}
-        x_tiles[0] = x_pool.tile([P, ROUND, K], BF16, name="x_tile")
-        load_sections(x_tiles[0], 0, ROUND)
-
+        for c in range(3):
+            x_tiles[c] = load_chunk(c)
         w_codes = const.tile([P, TAPS, 4 * C], U8, align_bytes=64)
         nc.sync.dma_start(
             out=w_codes[:].bitcast(I32),
@@ -135,62 +176,59 @@ def tile_predictor_pa_t_e_kernel(tc, x, W1_words, W1_scales, b1, out):
                 out=w_scales[32 * quadrant : 32 * quadrant + 4, :, :].bitcast(I32),
                 in_=scale_rows[4 * quadrant : 4 * quadrant + 4, :, :],
             )
-        for r in range(1, LOAD_AHEAD):
-            x_tiles[r] = x_pool.tile([P, ROUND, K], BF16, name="x_tile")
-            load_sections(x_tiles[r], r * ROUND, ROUND)
+        for c in range(3, LOAD_AHEAD):
+            x_tiles[c] = load_chunk(c)
 
         b1_rows = const.tile([P, C], BF16)
         nc.scalar.dma_start(out=b1_rows[:], in_=b1[0].partition_broadcast(P))
 
         identity = const.tile([P, P], F32)
         make_identity(nc, identity[:])
-        warm = const.tile([P, 1], F32)
-        nc.vector.memset(warm[:], 0.0)
-        nc.scalar.activation(out=warm[:], in_=warm[:], func=mybir.ActivationFunctionType.Tanh)
+        warm_col = const.tile([P, 1], F32)
+        nc.vector.memset(warm_col[:], 0.0)
+        nc.scalar.activation(out=warm_col[:], in_=warm_col[:], func=mybir.ActivationFunctionType.Tanh)
+        nc.vector.memset(halo_codes[:].bitcast(I32), 0)
+        nc.vector.memset(halo_scales[:].bitcast(I32), 0)
+        nc.vector.memset(x_scales[:, SECTIONS - HALO : SECTIONS, :].bitcast(I32), 0)
 
-        grouped_halo = const.tile([P, HALO, P, 4], BF16, align_bytes=64)
-        nc.vector.memset(grouped_halo[:], 0.0)
-        halo_sorted = const.tile([P, HALO, PAIRS, P], F32)
-        sort_sections(x_halo, halo_sorted)
-        transpose_sections(halo_sorted, grouped_halo, HALO, 1)
         sorted_tiles = {}
-        for r in range(SORT_AHEAD):
-            sorted_tiles[r] = sorted_pool.tile([P, ROUND, PAIRS, P], F32, name="x_sorted")
-            sort_sections(x_tiles[r], sorted_tiles[r])
-        quantise_sections(grouped_halo, 0, HALO)
+        for c in range(SORT_AHEAD):
+            sorted_tiles[c] = sort_chunk(c, x_tiles[c])
 
         bias_full = const.tile([P, ACC_SECTIONS, C], F32)
         bias_head = const.tile([P, ACC_SECTIONS, C], F32)
-        for q in range(ACC_SECTIONS):
-            nc.vector.tensor_scalar_mul(out=bias_full[:, q, :], in0=b1_rows[:], scalar1=float(TAPS))
-            nc.vector.tensor_scalar_mul(out=bias_head[:, q, :], in0=b1_rows[:], scalar1=float(TAPS))
-        for q in range(HALO):
-            nc.vector.tensor_scalar_mul(
-                out=bias_head[0:1, q, :], in0=b1_rows[0:1, :], scalar1=float(q + 1)
-            )
+        head_group = outputs[1][0:ACC_SECTIONS]
+        assert head_group[0:HALO] == list(range(HALO))
+
+        def make_bias():
+            for q in range(ACC_SECTIONS):
+                nc.vector.tensor_scalar_mul(out=bias_full[:, q, :], in0=b1_rows[:], scalar1=float(TAPS))
+                nc.vector.tensor_scalar_mul(out=bias_head[:, q, :], in0=b1_rows[:], scalar1=float(TAPS))
+            for t in range(HALO):
+                q = head_group.index(t)
+                nc.vector.tensor_scalar_mul(
+                    out=bias_head[0:1, q, :], in0=b1_rows[0:1, :], scalar1=float(t + 1)
+                )
 
         grouped_tiles = {}
         acc_banks = {}
         result_tiles = {}
-        for i in range(ROUNDS + 3):
-            if i + LOAD_AHEAD < ROUNDS:
-                x_tiles[i + LOAD_AHEAD] = x_pool.tile([P, ROUND, K], BF16, name="x_tile")
-                load_sections(x_tiles[i + LOAD_AHEAD], (i + LOAD_AHEAD) * ROUND, ROUND)
-            if 0 <= i - 3:
-                result_tiles[i - 3] = add_bias(i - 3, acc_banks[i - 3])
-            if 0 <= i - 1 < ROUNDS:
-                quantise_sections(grouped_tiles[i - 1], HALO + (i - 1) * ROUND, ROUND)
-            if i + SORT_AHEAD < ROUNDS:
-                sorted_tiles[i + SORT_AHEAD] = sorted_pool.tile(
-                    [P, ROUND, PAIRS, P], F32, name="x_sorted"
-                )
-                sort_sections(x_tiles[i + SORT_AHEAD], sorted_tiles[i + SORT_AHEAD])
-            if i < ROUNDS:
-                grouped_tiles[i] = grouped_pool.tile(
-                    [P, ROUND, P, 4], BF16, name="grouped", align_bytes=64
-                )
-                transpose_sections(sorted_tiles[i], grouped_tiles[i], ROUND, 0)
-            if 0 <= i - 2 < ROUNDS:
-                acc_banks[i - 2] = multiply_round(i - 2)
-            if 0 <= i - 3:
+        for i in range(n_chunks + 3):
+            if LOAD_AHEAD <= i + LOAD_AHEAD < n_chunks:
+                x_tiles[i + LOAD_AHEAD] = load_chunk(i + LOAD_AHEAD)
+            if 0 <= i - 3 and acc_banks[i - 3]:
+                result_tiles[i - 3] = add_bias(acc_banks[i - 3])
+            if 0 <= i - 1 < n_chunks:
+                quantise_chunk(i - 1, grouped_tiles[i - 1])
+                if i - 1 == 0:
+                    make_halo()
+            if SORT_AHEAD <= i + SORT_AHEAD < n_chunks:
+                sorted_tiles[i + SORT_AHEAD] = sort_chunk(i + SORT_AHEAD, x_tiles[i + SORT_AHEAD])
+            if i == 1:
+                make_bias()
+            if i < n_chunks:
+                grouped_tiles[i] = transpose_chunk(i, sorted_tiles[i])
+            if 0 <= i - 2 < n_chunks:
+                acc_banks[i - 2] = multiply_chunk(i - 2)
+            if 0 <= i - 3 and acc_banks[i - 3]:
                 tanh_and_store(i - 3, result_tiles[i - 3])

@@ -176,14 +176,17 @@ def tile_predictor_pa_t_e_kernel(tc, x, W1_words, W1_scales, b1, out):
                 out=w_scales[32 * quadrant : 32 * quadrant + 4, :, :].bitcast(I32),
                 in_=scale_rows[4 * quadrant : 4 * quadrant + 4, :, :],
             )
+        b1_row = const.tile([P, C], BF16)
+        nc.gpsimd.memset(b1_row[:], 0.0)
+        nc.sync.dma_start(out=b1_row[0:1, :], in_=b1)
         for c in range(3, LOAD_AHEAD):
             x_tiles[c] = load_chunk(c)
 
-        b1_rows = const.tile([P, C], BF16)
-        nc.scalar.dma_start(out=b1_rows[:], in_=b1[0].partition_broadcast(P))
 
         identity = const.tile([P, P], F32)
         make_identity(nc, identity[:])
+        ones = const.tile([P, P], BF16)
+        nc.gpsimd.memset(ones[:], 1.0)
         warm_col = const.tile([P, 1], F32)
         nc.vector.memset(warm_col[:], 0.0)
         nc.scalar.activation(out=warm_col[:], in_=warm_col[:], func=mybir.ActivationFunctionType.Tanh)
@@ -201,13 +204,15 @@ def tile_predictor_pa_t_e_kernel(tc, x, W1_words, W1_scales, b1, out):
         assert head_group[0:HALO] == list(range(HALO))
 
         def make_bias():
+            bias_bank = acc_pool.tile([P, ACC_SECTIONS, C], F32, name="acc")
             for q in range(ACC_SECTIONS):
-                nc.vector.tensor_scalar_mul(out=bias_full[:, q, :], in0=b1_rows[:], scalar1=float(TAPS))
-                nc.vector.tensor_scalar_mul(out=bias_head[:, q, :], in0=b1_rows[:], scalar1=float(TAPS))
+                nc.tensor.matmul(out=bias_bank[:, q, :], lhsT=ones[:], rhs=b1_row[:], start=True, stop=True)
+            nc.vector.tensor_scalar_mul(out=bias_full[:], in0=bias_bank[:], scalar1=float(TAPS))
+            nc.vector.tensor_scalar_mul(out=bias_head[:], in0=bias_bank[:], scalar1=float(TAPS))
             for t in range(HALO):
                 q = head_group.index(t)
                 nc.vector.tensor_scalar_mul(
-                    out=bias_head[0:1, q, :], in0=b1_rows[0:1, :], scalar1=float(t + 1)
+                    out=bias_head[0:1, q, :], in0=bias_bank[0:1, q, :], scalar1=float(t + 1)
                 )
 
         grouped_tiles = {}
@@ -224,11 +229,11 @@ def tile_predictor_pa_t_e_kernel(tc, x, W1_words, W1_scales, b1, out):
                     make_halo()
             if SORT_AHEAD <= i + SORT_AHEAD < n_chunks:
                 sorted_tiles[i + SORT_AHEAD] = sort_chunk(i + SORT_AHEAD, x_tiles[i + SORT_AHEAD])
-            if i == 1:
-                make_bias()
             if i < n_chunks:
                 grouped_tiles[i] = transpose_chunk(i, sorted_tiles[i])
             if 0 <= i - 2 < n_chunks:
                 acc_banks[i - 2] = multiply_chunk(i - 2)
+            if i == 2:
+                make_bias()
             if 0 <= i - 3 and acc_banks[i - 3]:
                 tanh_and_store(i - 3, result_tiles[i - 3])

@@ -136,11 +136,11 @@ def tile_predictor_pa_t_e_kernel(tc, x, W1_words, W1_scales, b1, out):
             result = result_pool.tile([P, most_outputs, C], F32, name="result")
             at = 0
             for acc, group in banks:
-                bias = bias_head if 0 in group else bias_full
+                counted = bias[:, 1 : 1 + HALO, :] if 0 in group else bias[:, 0:1, :].to_broadcast([P, len(group), C])
                 nc.vector.tensor_tensor(
                     out=result[:, at : at + len(group), :],
                     in0=acc[:, 0 : len(group), :],
-                    in1=bias[:, 0 : len(group), :],
+                    in1=counted,
                     op=mybir.AluOpType.add,
                 )
                 at += len(group)
@@ -161,7 +161,7 @@ def tile_predictor_pa_t_e_kernel(tc, x, W1_words, W1_scales, b1, out):
                 at += run
 
         x_tiles = {}
-        for c in range(3):
+        for c in range(4):
             x_tiles[c] = load_chunk(c)
         w_codes = const.tile([P, TAPS, 4 * C], U8, align_bytes=64)
         nc.sync.dma_start(
@@ -179,14 +179,16 @@ def tile_predictor_pa_t_e_kernel(tc, x, W1_words, W1_scales, b1, out):
         b1_row = const.tile([P, C], BF16)
         nc.gpsimd.memset(b1_row[:], 0.0)
         nc.sync.dma_start(out=b1_row[0:1, :], in_=b1)
-        for c in range(3, LOAD_AHEAD):
+        for c in range(4, LOAD_AHEAD):
             x_tiles[c] = load_chunk(c)
 
 
         identity = const.tile([P, P], F32)
         make_identity(nc, identity[:])
-        ones = const.tile([P, P], BF16)
-        nc.gpsimd.memset(ones[:], 1.0)
+        counts = const.tile([P, 1 + HALO, P], BF16)
+        nc.gpsimd.memset(counts[:], float(TAPS))
+        for t in range(HALO):
+            nc.gpsimd.memset(counts[:, 1 + t, 0:1], float(t + 1))
         warm_col = const.tile([P, 1], F32)
         nc.vector.memset(warm_col[:], 0.0)
         nc.scalar.activation(out=warm_col[:], in_=warm_col[:], func=mybir.ActivationFunctionType.Tanh)
@@ -198,22 +200,14 @@ def tile_predictor_pa_t_e_kernel(tc, x, W1_words, W1_scales, b1, out):
         for c in range(SORT_AHEAD):
             sorted_tiles[c] = sort_chunk(c, x_tiles[c])
 
-        bias_full = const.tile([P, ACC_SECTIONS, C], F32)
-        bias_head = const.tile([P, ACC_SECTIONS, C], F32)
-        head_group = outputs[1][0:ACC_SECTIONS]
-        assert head_group[0:HALO] == list(range(HALO))
+        bias = const.tile([P, 1 + HALO, C], F32)
+        assert outputs[1] == list(range(HALO))
 
         def make_bias():
             bias_bank = acc_pool.tile([P, ACC_SECTIONS, C], F32, name="acc")
-            for q in range(ACC_SECTIONS):
-                nc.tensor.matmul(out=bias_bank[:, q, :], lhsT=ones[:], rhs=b1_row[:], start=True, stop=True)
-            nc.vector.tensor_scalar_mul(out=bias_full[:], in0=bias_bank[:], scalar1=float(TAPS))
-            nc.vector.tensor_scalar_mul(out=bias_head[:], in0=bias_bank[:], scalar1=float(TAPS))
-            for t in range(HALO):
-                q = head_group.index(t)
-                nc.vector.tensor_scalar_mul(
-                    out=bias_head[0:1, q, :], in0=bias_bank[0:1, q, :], scalar1=float(t + 1)
-                )
+            for v in range(1 + HALO):
+                nc.tensor.matmul(out=bias_bank[:, v, :], lhsT=counts[:, v, :], rhs=b1_row[:], start=True, stop=True)
+            nc.scalar.copy(out=bias[:], in_=bias_bank[:, 0 : 1 + HALO, :])
 
         grouped_tiles = {}
         acc_banks = {}

@@ -19,10 +19,10 @@ HALO = TAPS - 1
 SECTIONS = ROWS // P
 PAIRS = 2
 
-CHUNKS = (2,2,4,8,8,8,8,8,8,8,8,8,8,8,8,8,8,4,2,2)
+CHUNKS = (2,2,4,4,6,6,6,6,6,6,6,6,6,6,6,6,6,6,6,6,6,6,4,2,2)
 XT_SECTIONS = 2
 ACC_SECTIONS = 4
-LOAD_AHEAD = 7
+LOAD_AHEAD = 9
 SORT_AHEAD = 2
 QUANTISE_WIDTHS = (8, 4, 2)
 
@@ -44,7 +44,7 @@ def tile_predictor_pa_t_e_kernel(tc, x, W1_words, W1_scales, b1, out):
 
     with ExitStack() as ctx:
         const = ctx.enter_context(tc.tile_pool(name="const", bufs=1))
-        x_pool = ctx.enter_context(tc.tile_pool(name="x_pool", bufs=7))
+        x_pool = ctx.enter_context(tc.tile_pool(name="x_pool", bufs=9))
         sorted_pool = ctx.enter_context(tc.tile_pool(name="sorted_pool", bufs=4))
         grouped_pool = ctx.enter_context(tc.tile_pool(name="grouped_pool", bufs=3))
         result_pool = ctx.enter_context(tc.tile_pool(name="result_pool", bufs=6))

@@ -24,6 +24,8 @@ XT_SECTIONS = 2
 ACC_SECTIONS = 4
 LOAD_AHEAD = 9
 SORT_AHEAD = 2
+UNSORTED = 2
+VECTOR_BANKS = ()
 QUANTISE_WIDTHS = (8, 4, 2)
 
 FLOPS = 2 * ROWS * TAPS * K * C
@@ -41,10 +43,11 @@ def tile_predictor_pa_t_e_kernel(tc, x, W1_words, W1_scales, b1, out):
     outputs[0] = []
     most_outputs = max(len(o) for o in outputs)
     most_sections = max(CHUNKS)
+    n_sorted = [n - UNSORTED if n == most_sections else n for n in CHUNKS]
 
     with ExitStack() as ctx:
         const = ctx.enter_context(tc.tile_pool(name="const", bufs=1))
-        x_pool = ctx.enter_context(tc.tile_pool(name="x_pool", bufs=9))
+        x_pool = ctx.enter_context(tc.tile_pool(name="x_pool", bufs=11))
         sorted_pool = ctx.enter_context(tc.tile_pool(name="sorted_pool", bufs=4))
         grouped_pool = ctx.enter_context(tc.tile_pool(name="grouped_pool", bufs=3))
         result_pool = ctx.enter_context(tc.tile_pool(name="result_pool", bufs=6))
@@ -65,25 +68,35 @@ def tile_predictor_pa_t_e_kernel(tc, x, W1_words, W1_scales, b1, out):
             return x_tile
 
         def sort_chunk(c, x_tile):
-            x_sorted = sorted_pool.tile([P, most_sections, PAIRS, P], F32, name="x_sorted")
+            x_sorted = sorted_pool.tile([P, max(n_sorted), PAIRS, P], F32, name="x_sorted")
             nc.vector.tensor_copy(
-                out=x_sorted[:, 0 : CHUNKS[c], :, :],
-                in_=x_tile[:, 0 : CHUNKS[c], :].bitcast(F32).rearrange("j s (p u) -> j s u p", u=PAIRS),
+                out=x_sorted[:, 0 : n_sorted[c], :, :],
+                in_=x_tile[:, 0 : n_sorted[c], :].bitcast(F32).rearrange("j s (p u) -> j s u p", u=PAIRS),
             )
             return x_sorted
 
-        def transpose_chunk(c, x_sorted):
+        def transpose_chunk(c, x_sorted, x_tile):
             grouped = grouped_pool.tile([P, most_sections, P, 4], BF16, name="grouped", align_bytes=64)
             words_out = grouped[:].bitcast(F32)
             for first in range(0, CHUNKS[c], XT_SECTIONS):
                 xt = xt_pool.tile([P, XT_SECTIONS, PAIRS, P], F32, name="xt")
                 for s in range(XT_SECTIONS):
                     for u in range(PAIRS):
-                        nc.tensor.transpose(xt[:, s, u, :], x_sorted[:, first + s, u, :], identity[:])
-                nc.scalar.copy(
-                    out=words_out[:, first : first + XT_SECTIONS, :, :],
-                    in_=xt[:].rearrange("p s u j -> p s j u"),
-                )
+                        if first + s < n_sorted[c]:
+                            words = x_sorted[:, first + s, u, :]
+                        else:
+                            words = x_tile[:, first + s, :].bitcast(F32)[:, u : K // 2 : PAIRS]
+                        nc.tensor.transpose(xt[:, s, u, :], words, identity[:])
+                if CHUNKS[c] == most_sections and first // XT_SECTIONS in VECTOR_BANKS:
+                    nc.vector.tensor_copy(
+                        out=words_out[:, first : first + XT_SECTIONS, :, :],
+                        in_=xt[:].rearrange("p s u j -> p s j u"),
+                    )
+                else:
+                    nc.scalar.copy(
+                        out=words_out[:, first : first + XT_SECTIONS, :, :],
+                        in_=xt[:].rearrange("p s u j -> p s j u"),
+                    )
             return grouped
 
         def quantise_chunk(c, grouped):
@@ -224,7 +237,7 @@ def tile_predictor_pa_t_e_kernel(tc, x, W1_words, W1_scales, b1, out):
             if SORT_AHEAD <= i + SORT_AHEAD < n_chunks:
                 sorted_tiles[i + SORT_AHEAD] = sort_chunk(i + SORT_AHEAD, x_tiles[i + SORT_AHEAD])
             if i < n_chunks:
-                grouped_tiles[i] = transpose_chunk(i, sorted_tiles[i])
+                grouped_tiles[i] = transpose_chunk(i, sorted_tiles[i], x_tiles[i])
             if 0 <= i - 2 < n_chunks:
                 acc_banks[i - 2] = multiply_chunk(i - 2)
             if i == 2:

@@ -24,7 +24,7 @@ XT_SECTIONS = 2
 ACC_SECTIONS = 4
 LOAD_AHEAD = 9
 SORT_AHEAD = 2
-UNSORTED = 2
+UNSORTED = 1
 VECTOR_BANKS = ()
 QUANTISE_WIDTHS = (8, 4, 2)
 
@@ -68,10 +68,10 @@ def tile_predictor_pa_t_e_kernel(tc, x, W1_words, W1_scales, b1, out):
             return x_tile
 
         def sort_chunk(c, x_tile):
-            x_sorted = sorted_pool.tile([P, max(n_sorted), PAIRS, P], F32, name="x_sorted")
+            x_sorted = sorted_pool.tile([P, PAIRS, max(n_sorted), P], F32, name="x_sorted")
             nc.vector.tensor_copy(
-                out=x_sorted[:, 0 : n_sorted[c], :, :],
-                in_=x_tile[:, 0 : n_sorted[c], :].bitcast(F32).rearrange("j s (p u) -> j s u p", u=PAIRS),
+                out=x_sorted[:, :, 0 : n_sorted[c], :],
+                in_=x_tile[:, 0 : n_sorted[c], :].bitcast(F32).rearrange("j s (p u) -> j u s p", u=PAIRS),
             )
             return x_sorted
 
@@ -83,7 +83,7 @@ def tile_predictor_pa_t_e_kernel(tc, x, W1_words, W1_scales, b1, out):
                 for s in range(XT_SECTIONS):
                     for u in range(PAIRS):
                         if first + s < n_sorted[c]:
-                            words = x_sorted[:, first + s, u, :]
+                            words = x_sorted[:, u, first + s, :]
                         else:
                             words = x_tile[:, first + s, :].bitcast(F32)[:, u : K // 2 : PAIRS]
                         nc.tensor.transpose(xt[:, s, u, :], words, identity[:])

@@ -125,24 +125,28 @@ def tile_predictor_pa_t_e_kernel(tc, x, W1_words, W1_scales, b1, out):
                 return halo_codes[:, HALO + t, :], halo_scales[:, HALO + t, :]
             return x_codes[:, t, :], x_scales[:, t, :]
 
+        def multiply_pair(acc, q, t):
+            passes = ((t, 0, 0, 2), (t + 1, 0, 1, 1), (t - 2, 2, 0, 1), (t - 1, 1, 0, 2))
+            for n, (section, tap, place, width) in enumerate(passes):
+                codes, scales = stationary(section)
+                nc.tensor.matmul_mx(
+                    out=acc[:, q + place : q + place + width, :].rearrange("p s c -> p (s c)"),
+                    lhsT=codes.bitcast(FP8X4),
+                    lhsT_scale=scales,
+                    rhs=w_codes[:, tap : tap + width, :].rearrange("p g n -> p (g n)").bitcast(FP8X4),
+                    rhs_scale=w_scales[:, tap : tap + width, :].rearrange("p g n -> p (g n)"),
+                    start=(n == 0),
+                    stop=(n == len(passes) - 1),
+                )
+
         def multiply_chunk(c):
             banks = []
             for g in range(0, len(outputs[c]), ACC_SECTIONS):
                 group = outputs[c][g : g + ACC_SECTIONS]
                 acc = acc_pool.tile([P, ACC_SECTIONS, C], F32, name="acc")
                 banks.append((acc, group))
-                for q in range(len(group)):
-                    for tap in range(TAPS):
-                        codes, scales = stationary(group[q] - tap)
-                        nc.tensor.matmul_mx(
-                            out=acc[:, q, :],
-                            lhsT=codes.bitcast(FP8X4),
-                            lhsT_scale=scales,
-                            rhs=w_codes[:, tap, :].bitcast(FP8X4),
-                            rhs_scale=w_scales[:, tap, :],
-                            start=(tap == 0),
-                            stop=(tap == TAPS - 1),
-                        )
+                for q in range(0, len(group), 2):
+                    multiply_pair(acc, q, group[q])
             return banks
 
         def add_bias(banks):

@@ -19,7 +19,7 @@ HALO = TAPS - 1
 SECTIONS = ROWS // P
 PAIRS = 2
 
-CHUNKS = (2,2,4,4,6,6,6,6,6,6,6,6,6,6,6,6,6,6,6,6,6,6,4,2,2)
+CHUNKS = (2, 2, 4, 4) + (6,) * 19 + (2,)
 XT_SECTIONS = 2
 ACC_SECTIONS = 4
 LOAD_AHEAD = 9
@@ -50,7 +50,7 @@ def tile_predictor_pa_t_e_kernel(tc, x, W1_words, W1_scales, b1, out):
         x_pool = ctx.enter_context(tc.tile_pool(name="x_pool", bufs=11))
         sorted_pool = ctx.enter_context(tc.tile_pool(name="sorted_pool", bufs=4))
         grouped_pool = ctx.enter_context(tc.tile_pool(name="grouped_pool", bufs=3))
-        result_pool = ctx.enter_context(tc.tile_pool(name="result_pool", bufs=6))
+        result_pool = ctx.enter_context(tc.tile_pool(name="result_pool", bufs=12))
         xt_pool = ctx.enter_context(tc.psum_pool(name="xt_pool", bufs=4))
         acc_pool = ctx.enter_context(tc.psum_pool(name="acc_pool", bufs=4))
         ctx.enter_context(tc.manual_schedule())
@@ -178,13 +178,15 @@ def tile_predictor_pa_t_e_kernel(tc, x, W1_words, W1_scales, b1, out):
                 at += run
 
         x_tiles = {}
-        for c in range(4):
+        for c in range(3):
             x_tiles[c] = load_chunk(c)
         w_codes = const.tile([P, TAPS, 4 * C], U8, align_bytes=64)
         nc.sync.dma_start(
             out=w_codes[:].bitcast(I32),
             in_=W1_words.rearrange("g p n t -> p g (n t)").bitcast(I32),
         )
+        for c in range(3, 5):
+            x_tiles[c] = load_chunk(c)
         w_scales = const.tile([P, TAPS, C], U8, align_bytes=64)
         nc.vector.memset(w_scales[:].bitcast(I32), 0)
         scale_rows = W1_scales.bitcast(I32).rearrange("g q n -> q g n")
@@ -196,7 +198,7 @@ def tile_predictor_pa_t_e_kernel(tc, x, W1_words, W1_scales, b1, out):
         b1_row = const.tile([P, C], BF16)
         nc.gpsimd.memset(b1_row[:], 0.0)
         nc.sync.dma_start(out=b1_row[0:1, :], in_=b1)
-        for c in range(4, LOAD_AHEAD):
+        for c in range(5, LOAD_AHEAD):
             x_tiles[c] = load_chunk(c)
 
 
@@ -242,9 +244,9 @@ def tile_predictor_pa_t_e_kernel(tc, x, W1_words, W1_scales, b1, out):
                 sorted_tiles[i + SORT_AHEAD] = sort_chunk(i + SORT_AHEAD, x_tiles[i + SORT_AHEAD])
             if i < n_chunks:
                 grouped_tiles[i] = transpose_chunk(i, sorted_tiles[i], x_tiles[i])
+            if i == 3:
+                make_bias()
             if 0 <= i - 2 < n_chunks:
                 acc_banks[i - 2] = multiply_chunk(i - 2)
-            if i == 2:
-                make_bias()
             if 0 <= i - 3 and acc_banks[i - 3]:
                 tanh_and_store(i - 3, result_tiles[i - 3])

@@ -22,7 +22,10 @@ PAIRS = 2
 CHUNKS = (2, 2, 4, 4) + (6,) * 19 + (2,)
 XT_SECTIONS = 2
 ACC_SECTIONS = 4
-LOAD_AHEAD = 9
+GROUP_SECTIONS = 12
+GROUPS_AHEAD = 5
+SPLIT_LOADS = 2
+SPLIT_STORES = 2
 SORT_AHEAD = 2
 UNSORTED = 1
 VECTOR_BANKS = ()
@@ -41,16 +44,19 @@ def tile_predictor_pa_t_e_kernel(tc, x, W1_words, W1_scales, b1, out):
     outputs = [list(range(firsts[c], firsts[c] + CHUNKS[c])) for c in range(n_chunks)]
     outputs[n_chunks - 1].extend(outputs[0])
     outputs[0] = []
-    most_outputs = max(len(o) for o in outputs)
+    group_of = [sum(CHUNKS[:c]) // GROUP_SECTIONS for c in range(n_chunks)]
+    place_of = [sum(CHUNKS[:c]) % GROUP_SECTIONS for c in range(n_chunks)]
+    n_groups = group_of[n_chunks - 1] + 1
+    members = [[c for c in range(n_chunks) if group_of[c] == g] for g in range(n_groups)]
     most_sections = max(CHUNKS)
     n_sorted = [n - UNSORTED if n == most_sections else n for n in CHUNKS]
 
     with ExitStack() as ctx:
         const = ctx.enter_context(tc.tile_pool(name="const", bufs=1))
-        x_pool = ctx.enter_context(tc.tile_pool(name="x_pool", bufs=11))
+        x_pool = ctx.enter_context(tc.tile_pool(name="x_pool", bufs=1 + GROUPS_AHEAD))
         sorted_pool = ctx.enter_context(tc.tile_pool(name="sorted_pool", bufs=4))
         grouped_pool = ctx.enter_context(tc.tile_pool(name="grouped_pool", bufs=3))
-        result_pool = ctx.enter_context(tc.tile_pool(name="result_pool", bufs=12))
+        result_pool = ctx.enter_context(tc.tile_pool(name="result_pool", bufs=5))
         xt_pool = ctx.enter_context(tc.psum_pool(name="xt_pool", bufs=4))
         acc_pool = ctx.enter_context(tc.psum_pool(name="acc_pool", bufs=4))
         ctx.enter_context(tc.manual_schedule())
@@ -60,22 +66,34 @@ def tile_predictor_pa_t_e_kernel(tc, x, W1_words, W1_scales, b1, out):
         halo_codes = const.tile([P, HALO, P], U32, align_bytes=64)
         halo_scales = const.tile([P, HALO, P], U8, align_bytes=64)
 
-        def load_chunk(c):
-            x_tile = x_pool.tile([P, most_sections, K], BF16, name="x_tile")
-            nc.sync.dma_start(
-                out=x_tile[:, 0 : CHUNKS[c], :], in_=x_sections[:, firsts[c] : firsts[c] + CHUNKS[c], :]
-            )
-            return x_tile
+        x_tiles = {}
+        result_group = {}
 
-        def sort_chunk(c, x_tile):
+        def load_sections(g, first_chunk, last_chunk):
+            if g not in x_tiles:
+                x_tiles[g] = x_pool.tile([P, GROUP_SECTIONS, K], BF16, name="x_tile")
+            count = sum(CHUNKS[first_chunk : last_chunk + 1])
+            place, t = place_of[first_chunk], firsts[first_chunk]
+            nc.sync.dma_start(out=x_tiles[g][:, place : place + count, :], in_=x_sections[:, t : t + count, :])
+
+        def load_chunk(c):
+            load_sections(group_of[c], c, c)
+
+        def load_group(g):
+            load_sections(g, members[g][0], members[g][-1])
+
+        def x_of(c):
+            return x_tiles[group_of[c]][:, place_of[c] : place_of[c] + CHUNKS[c], :]
+
+        def sort_chunk(c):
             x_sorted = sorted_pool.tile([P, PAIRS, max(n_sorted), P], F32, name="x_sorted")
             nc.vector.tensor_copy(
                 out=x_sorted[:, :, 0 : n_sorted[c], :],
-                in_=x_tile[:, 0 : n_sorted[c], :].bitcast(F32).rearrange("j s (p u) -> j u s p", u=PAIRS),
+                in_=x_of(c)[:, 0 : n_sorted[c], :].bitcast(F32).rearrange("j s (p u) -> j u s p", u=PAIRS),
             )
             return x_sorted
 
-        def transpose_chunk(c, x_sorted, x_tile):
+        def transpose_chunk(c, x_sorted):
             grouped = grouped_pool.tile([P, most_sections, P, 4], BF16, name="grouped", align_bytes=64)
             words_out = grouped[:].bitcast(F32)
             for first in range(0, CHUNKS[c], XT_SECTIONS):
@@ -85,7 +103,7 @@ def tile_predictor_pa_t_e_kernel(tc, x, W1_words, W1_scales, b1, out):
                         if first + s < n_sorted[c]:
                             words = x_sorted[:, u, first + s, :]
                         else:
-                            words = x_tile[:, first + s, :].bitcast(F32)[:, u : K // 2 : PAIRS]
+                            words = x_of(c)[:, first + s, :].bitcast(F32)[:, u : K // 2 : PAIRS]
                         nc.tensor.transpose(xt[:, s, u, :], words, identity[:])
                 if CHUNKS[c] == most_sections and first // XT_SECTIONS in VECTOR_BANKS:
                     nc.vector.tensor_copy(
@@ -149,9 +167,14 @@ def tile_predictor_pa_t_e_kernel(tc, x, W1_words, W1_scales, b1, out):
                     multiply_pair(acc, q, group[q])
             return banks
 
-        def add_bias(banks):
-            result = result_pool.tile([P, most_outputs, C], F32, name="result")
-            at = 0
+        def result_place(c):
+            return sum(len(outputs[m]) for m in members[group_of[c]] if m < c)
+
+        def add_bias(c, banks):
+            if group_of[c] not in result_group:
+                result_group[group_of[c]] = result_pool.tile([P, GROUP_SECTIONS, C], F32, name="result")
+            result = result_group[group_of[c]]
+            at = result_place(c)
             for acc, group in banks:
                 counted = bias[:, 1 : 1 + HALO, :] if 0 in group else bias[:, 0:1, :].to_broadcast([P, len(group), C])
                 nc.vector.tensor_tensor(
@@ -161,32 +184,30 @@ def tile_predictor_pa_t_e_kernel(tc, x, W1_words, W1_scales, b1, out):
                     op=mybir.AluOpType.add,
                 )
                 at += len(group)
-            return result
 
-        def tanh_and_store(c, result):
-            count = len(outputs[c])
-            nc.scalar.activation(
-                out=result[:, 0:count, :], in_=result[:, 0:count, :], func=mybir.ActivationFunctionType.Tanh
-            )
-            at = 0
-            while at < count:
-                run = 1
-                while at + run < count and outputs[c][at + run] == outputs[c][at] + run:
-                    run += 1
-                t = outputs[c][at]
-                nc.sync.dma_start(out=out_sections[:, t : t + run, :], in_=result[:, at : at + run, :])
-                at += run
+        def tanh_and_store(c):
+            g = group_of[c]
+            at, count = result_place(c), len(outputs[c])
+            done = result_group[g][:, at : at + count, :]
+            nc.scalar.activation(out=done, in_=done, func=mybir.ActivationFunctionType.Tanh)
+            if g >= n_groups - SPLIT_STORES:
+                first, t = at, outputs[c][0]
+            elif c == members[g][-1]:
+                first, t = 0, min(outputs[m][0] for m in members[g] if outputs[m])
+            else:
+                return
+            run = at + count - first
+            nc.sync.dma_start(out=out_sections[:, t : t + run, :], in_=result_group[g][:, first : first + run, :])
 
-        x_tiles = {}
         for c in range(3):
-            x_tiles[c] = load_chunk(c)
+            load_chunk(c)
         w_codes = const.tile([P, TAPS, 4 * C], U8, align_bytes=64)
         nc.sync.dma_start(
             out=w_codes[:].bitcast(I32),
             in_=W1_words.rearrange("g p n t -> p g (n t)").bitcast(I32),
         )
         for c in range(3, 5):
-            x_tiles[c] = load_chunk(c)
+            load_chunk(c)
         w_scales = const.tile([P, TAPS, C], U8, align_bytes=64)
         nc.vector.memset(w_scales[:].bitcast(I32), 0)
         scale_rows = W1_scales.bitcast(I32).rearrange("g q n -> q g n")
@@ -198,8 +219,10 @@ def tile_predictor_pa_t_e_kernel(tc, x, W1_words, W1_scales, b1, out):
         b1_row = const.tile([P, C], BF16)
         nc.gpsimd.memset(b1_row[:], 0.0)
         nc.sync.dma_start(out=b1_row[0:1, :], in_=b1)
-        for c in range(5, LOAD_AHEAD):
-            x_tiles[c] = load_chunk(c)
+        for c in range(5, members[SPLIT_LOADS][0]):
+            load_chunk(c)
+        for g in range(SPLIT_LOADS, GROUPS_AHEAD):
+            load_group(g)
 
 
         identity = const.tile([P, P], F32)
@@ -217,7 +240,7 @@ def tile_predictor_pa_t_e_kernel(tc, x, W1_words, W1_scales, b1, out):
 
         sorted_tiles = {}
         for c in range(SORT_AHEAD):
-            sorted_tiles[c] = sort_chunk(c, x_tiles[c])
+            sorted_tiles[c] = sort_chunk(c)
 
         bias = const.tile([P, 1 + HALO, C], F32)
         assert outputs[1] == list(range(HALO))
@@ -230,23 +253,22 @@ def tile_predictor_pa_t_e_kernel(tc, x, W1_words, W1_scales, b1, out):
 
         grouped_tiles = {}
         acc_banks = {}
-        result_tiles = {}
         for i in range(n_chunks + 3):
-            if LOAD_AHEAD <= i + LOAD_AHEAD < n_chunks:
-                x_tiles[i + LOAD_AHEAD] = load_chunk(i + LOAD_AHEAD)
+            if i < n_chunks and i == members[group_of[i]][0] and group_of[i] + GROUPS_AHEAD < n_groups:
+                load_group(group_of[i] + GROUPS_AHEAD)
             if 0 <= i - 3 and acc_banks[i - 3]:
-                result_tiles[i - 3] = add_bias(acc_banks[i - 3])
+                add_bias(i - 3, acc_banks[i - 3])
             if 0 <= i - 1 < n_chunks:
                 quantise_chunk(i - 1, grouped_tiles[i - 1])
                 if i - 1 == 0:
                     make_halo()
             if SORT_AHEAD <= i + SORT_AHEAD < n_chunks:
-                sorted_tiles[i + SORT_AHEAD] = sort_chunk(i + SORT_AHEAD, x_tiles[i + SORT_AHEAD])
+                sorted_tiles[i + SORT_AHEAD] = sort_chunk(i + SORT_AHEAD)
             if i < n_chunks:
-                grouped_tiles[i] = transpose_chunk(i, sorted_tiles[i], x_tiles[i])
+                grouped_tiles[i] = transpose_chunk(i, sorted_tiles[i])
             if i == 3:
                 make_bias()
             if 0 <= i - 2 < n_chunks:
                 acc_banks[i - 2] = multiply_chunk(i - 2)
             if 0 <= i - 3 and acc_banks[i - 3]:
-                tanh_and_store(i - 3, result_tiles[i - 3])
+                tanh_and_store(i - 3)

@@ -24,8 +24,9 @@ XT_SECTIONS = 2
 ACC_SECTIONS = 4
 GROUP_SECTIONS = 12
 GROUPS_AHEAD = 5
-SPLIT_LOADS = 2
+SPLIT_LOADS = 3
 SPLIT_STORES = 2
+BANK_STORES = 3
 SORT_AHEAD = 2
 UNSORTED = 1
 VECTOR_BANKS = ()
@@ -49,6 +50,7 @@ def tile_predictor_pa_t_e_kernel(tc, x, W1_words, W1_scales, b1, out):
     n_groups = group_of[n_chunks - 1] + 1
     members = [[c for c in range(n_chunks) if group_of[c] == g] for g in range(n_groups)]
     most_sections = max(CHUNKS)
+    bank_sections = [ACC_SECTIONS if c < n_chunks - 1 else 2 for c in range(n_chunks)]
     n_sorted = [n - UNSORTED if n == most_sections else n for n in CHUNKS]
 
     with ExitStack() as ctx:
@@ -159,8 +161,9 @@ def tile_predictor_pa_t_e_kernel(tc, x, W1_words, W1_scales, b1, out):
 
         def multiply_chunk(c):
             banks = []
-            for g in range(0, len(outputs[c]), ACC_SECTIONS):
-                group = outputs[c][g : g + ACC_SECTIONS]
+            size = bank_sections[c]
+            for g in range(0, len(outputs[c]), size):
+                group = outputs[c][g : g + size]
                 acc = acc_pool.tile([P, ACC_SECTIONS, C], F32, name="acc")
                 banks.append((acc, group))
                 for q in range(0, len(group), 2):
@@ -187,17 +190,21 @@ def tile_predictor_pa_t_e_kernel(tc, x, W1_words, W1_scales, b1, out):
 
         def tanh_and_store(c):
             g = group_of[c]
-            at, count = result_place(c), len(outputs[c])
-            done = result_group[g][:, at : at + count, :]
-            nc.scalar.activation(out=done, in_=done, func=mybir.ActivationFunctionType.Tanh)
-            if g >= n_groups - SPLIT_STORES:
-                first, t = at, outputs[c][0]
+            place = result_place(c)
+            if c >= n_chunks - BANK_STORES:
+                parts = [outputs[c][p : p + bank_sections[c]] for p in range(0, len(outputs[c]), bank_sections[c])]
+            elif g >= n_groups - SPLIT_STORES:
+                parts = [outputs[c]]
             elif c == members[g][-1]:
-                first, t = 0, min(outputs[m][0] for m in members[g] if outputs[m])
+                parts = [[t for m in members[g] for t in outputs[m]]]
+                place = 0
             else:
                 return
-            run = at + count - first
-            nc.sync.dma_start(out=out_sections[:, t : t + run, :], in_=result_group[g][:, first : first + run, :])
+            for part in parts:
+                done = result_group[g][:, place : place + len(part), :]
+                nc.scalar.activation(out=done, in_=done, func=mybir.ActivationFunctionType.Tanh)
+                nc.sync.dma_start(out=out_sections[:, part[0] : part[0] + len(part), :], in_=done)
+                place += len(part)
 
         for c in range(3):
             load_chunk(c)

from contextlib import ExitStack

import concourse.mybir as mybir
from concourse.masks import make_identity

F32 = mybir.dt.float32
BF16 = mybir.dt.bfloat16
I32 = mybir.dt.int32
U32 = mybir.dt.uint32
U8 = mybir.dt.uint8
FP8X4 = mybir.dt.float8_e4m3fn_x4

P = 128
ROWS = 16384
K = 512
C = 128
TAPS = 3
HALO = TAPS - 1
SECTIONS = ROWS // P
PAIRS = 2

CHUNKS = (2, 2, 4, 4) + (6,) * 19 + (2,)
XT_SECTIONS = 2
ACC_SECTIONS = 4
GROUP_SECTIONS = 12
GROUPS_AHEAD = 5
SPLIT_LOADS = 3
SPLIT_STORES = 2
BANK_STORES = 3
SORT_AHEAD = 2
UNSORTED = 1
VECTOR_BANKS = ()
QUANTISE_WIDTHS = (8, 4, 2)

FLOPS = 2 * ROWS * TAPS * K * C


def tile_predictor_pa_t_e_kernel(tc, x, W1_words, W1_scales, b1, out):
    nc = tc.nc
    x_sections = x.rearrange("(j t) k -> j t k", t=SECTIONS)
    out_sections = out.rearrange("(j t) c -> j t c", t=SECTIONS)
    n_chunks = len(CHUNKS)
    assert sum(CHUNKS) == SECTIONS and CHUNKS[0] == HALO
    firsts = [(sum(CHUNKS[:c]) - HALO) % SECTIONS for c in range(n_chunks)]
    outputs = [list(range(firsts[c], firsts[c] + CHUNKS[c])) for c in range(n_chunks)]
    outputs[n_chunks - 1].extend(outputs[0])
    outputs[0] = []
    group_of = [sum(CHUNKS[:c]) // GROUP_SECTIONS for c in range(n_chunks)]
    place_of = [sum(CHUNKS[:c]) % GROUP_SECTIONS for c in range(n_chunks)]
    n_groups = group_of[n_chunks - 1] + 1
    members = [[c for c in range(n_chunks) if group_of[c] == g] for g in range(n_groups)]
    most_sections = max(CHUNKS)
    bank_sections = [ACC_SECTIONS if c < n_chunks - 1 else 2 for c in range(n_chunks)]
    n_sorted = [n - UNSORTED if n == most_sections else n for n in CHUNKS]

    with ExitStack() as ctx:
        const = ctx.enter_context(tc.tile_pool(name="const", bufs=1))
        x_pool = ctx.enter_context(tc.tile_pool(name="x_pool", bufs=1 + GROUPS_AHEAD))
        sorted_pool = ctx.enter_context(tc.tile_pool(name="sorted_pool", bufs=4))
        grouped_pool = ctx.enter_context(tc.tile_pool(name="grouped_pool", bufs=3))
        result_pool = ctx.enter_context(tc.tile_pool(name="result_pool", bufs=5))
        xt_pool = ctx.enter_context(tc.psum_pool(name="xt_pool", bufs=4))
        acc_pool = ctx.enter_context(tc.psum_pool(name="acc_pool", bufs=4))
        ctx.enter_context(tc.manual_schedule())

        x_codes = const.tile([P, SECTIONS, P], U32, align_bytes=64)
        x_scales = const.tile([P, SECTIONS, P], U8, align_bytes=64)
        halo_codes = const.tile([P, HALO, P], U32, align_bytes=64)
        halo_scales = const.tile([P, HALO, P], U8, align_bytes=64)

        x_tiles = {}
        result_group = {}

        def load_sections(g, first_chunk, last_chunk):
            if g not in x_tiles:
                x_tiles[g] = x_pool.tile([P, GROUP_SECTIONS, K], BF16, name="x_tile")
            count = sum(CHUNKS[first_chunk : last_chunk + 1])
            place, t = place_of[first_chunk], firsts[first_chunk]
            nc.sync.dma_start(out=x_tiles[g][:, place : place + count, :], in_=x_sections[:, t : t + count, :])

        def load_chunk(c):
            load_sections(group_of[c], c, c)

        def load_group(g):
            load_sections(g, members[g][0], members[g][-1])

        def x_of(c):
            return x_tiles[group_of[c]][:, place_of[c] : place_of[c] + CHUNKS[c], :]

        def sort_chunk(c):
            x_sorted = sorted_pool.tile([P, PAIRS, max(n_sorted), P], F32, name="x_sorted")
            nc.vector.tensor_copy(
                out=x_sorted[:, :, 0 : n_sorted[c], :],
                in_=x_of(c)[:, 0 : n_sorted[c], :].bitcast(F32).rearrange("j s (p u) -> j u s p", u=PAIRS),
            )
            return x_sorted

        def transpose_chunk(c, x_sorted):
            grouped = grouped_pool.tile([P, most_sections, P, 4], BF16, name="grouped", align_bytes=64)
            words_out = grouped[:].bitcast(F32)
            for first in range(0, CHUNKS[c], XT_SECTIONS):
                xt = xt_pool.tile([P, XT_SECTIONS, PAIRS, P], F32, name="xt")
                for s in range(XT_SECTIONS):
                    for u in range(PAIRS):
                        if first + s < n_sorted[c]:
                            words = x_sorted[:, u, first + s, :]
                        else:
                            words = x_of(c)[:, first + s, :].bitcast(F32)[:, u : K // 2 : PAIRS]
                        nc.tensor.transpose(xt[:, s, u, :], words, identity[:])
                if CHUNKS[c] == most_sections and first // XT_SECTIONS in VECTOR_BANKS:
                    nc.vector.tensor_copy(
                        out=words_out[:, first : first + XT_SECTIONS, :, :],
                        in_=xt[:].rearrange("p s u j -> p s j u"),
                    )
                else:
                    nc.scalar.copy(
                        out=words_out[:, first : first + XT_SECTIONS, :, :],
                        in_=xt[:].rearrange("p s u j -> p s j u"),
                    )
            return grouped

        def quantise_chunk(c, grouped):
            done = 0
            while done < CHUNKS[c]:
                count = max(w for w in QUANTISE_WIDTHS if w <= CHUNKS[c] - done)
                t = firsts[c] + done
                nc.vector.quantize_mx(
                    out=x_codes[:, t : t + count, :].rearrange("p s j -> p (s j)").bitcast(FP8X4),
                    scales=x_scales[:, t : t + count, :].rearrange("p s j -> p (s j)"),
                    in_=grouped[:, done : done + count, :, :].rearrange("p s j t -> p (s j t)"),
                )
                done += count

        def make_halo():
            nc.vector.tensor_copy(
                out=halo_codes[:, :, 1:P].bitcast(I32),
                in_=x_codes[:, SECTIONS - HALO : SECTIONS, 0 : P - 1].bitcast(I32),
            )
            nc.vector.tensor_copy(
                out=halo_scales[:, :, 1:P], in_=x_scales[:, SECTIONS - HALO : SECTIONS, 0 : P - 1]
            )

        def stationary(t):
            if t < 0:
                return halo_codes[:, HALO + t, :], halo_scales[:, HALO + t, :]
            return x_codes[:, t, :], x_scales[:, t, :]

        def multiply_pair(acc, q, t):
            passes = ((t, 0, 0, 2), (t + 1, 0, 1, 1), (t - 2, 2, 0, 1), (t - 1, 1, 0, 2))
            for n, (section, tap, place, width) in enumerate(passes):
                codes, scales = stationary(section)
                nc.tensor.matmul_mx(
                    out=acc[:, q + place : q + place + width, :].rearrange("p s c -> p (s c)"),
                    lhsT=codes.bitcast(FP8X4),
                    lhsT_scale=scales,
                    rhs=w_codes[:, tap : tap + width, :].rearrange("p g n -> p (g n)").bitcast(FP8X4),
                    rhs_scale=w_scales[:, tap : tap + width, :].rearrange("p g n -> p (g n)"),
                    start=(n == 0),
                    stop=(n == len(passes) - 1),
                )

        def multiply_chunk(c):
            banks = []
            size = bank_sections[c]
            for g in range(0, len(outputs[c]), size):
                group = outputs[c][g : g + size]
                acc = acc_pool.tile([P, ACC_SECTIONS, C], F32, name="acc")
                banks.append((acc, group))
                for q in range(0, len(group), 2):
                    multiply_pair(acc, q, group[q])
            return banks

        def result_place(c):
            return sum(len(outputs[m]) for m in members[group_of[c]] if m < c)

        def add_bias(c, banks):
            if group_of[c] not in result_group:
                result_group[group_of[c]] = result_pool.tile([P, GROUP_SECTIONS, C], F32, name="result")
            result = result_group[group_of[c]]
            at = result_place(c)
            for acc, group in banks:
                counted = bias[:, 1 : 1 + HALO, :] if 0 in group else bias[:, 0:1, :].to_broadcast([P, len(group), C])
                nc.vector.tensor_tensor(
                    out=result[:, at : at + len(group), :],
                    in0=acc[:, 0 : len(group), :],
                    in1=counted,
                    op=mybir.AluOpType.add,
                )
                at += len(group)

        def tanh_and_store(c):
            g = group_of[c]
            place = result_place(c)
            if c >= n_chunks - BANK_STORES:
                parts = [outputs[c][p : p + bank_sections[c]] for p in range(0, len(outputs[c]), bank_sections[c])]
            elif g >= n_groups - SPLIT_STORES:
                parts = [outputs[c]]
            elif c == members[g][-1]:
                parts = [[t for m in members[g] for t in outputs[m]]]
                place = 0
            else:
                return
            for part in parts:
                done = result_group[g][:, place : place + len(part), :]
                nc.scalar.activation(out=done, in_=done, func=mybir.ActivationFunctionType.Tanh)
                nc.sync.dma_start(out=out_sections[:, part[0] : part[0] + len(part), :], in_=done)
                place += len(part)

        for c in range(3):
            load_chunk(c)
        w_codes = const.tile([P, TAPS, 4 * C], U8, align_bytes=64)
        nc.sync.dma_start(
            out=w_codes[:].bitcast(I32),
            in_=W1_words.rearrange("g p n t -> p g (n t)").bitcast(I32),
        )
        for c in range(3, 5):
            load_chunk(c)
        w_scales = const.tile([P, TAPS, C], U8, align_bytes=64)
        nc.vector.memset(w_scales[:].bitcast(I32), 0)
        scale_rows = W1_scales.bitcast(I32).rearrange("g q n -> q g n")
        for quadrant in range(4):
            nc.sync.dma_start(
                out=w_scales[32 * quadrant : 32 * quadrant + 4, :, :].bitcast(I32),
                in_=scale_rows[4 * quadrant : 4 * quadrant + 4, :, :],
            )
        b1_row = const.tile([P, C], BF16)
        nc.gpsimd.memset(b1_row[:], 0.0)
        nc.sync.dma_start(out=b1_row[0:1, :], in_=b1)
        for c in range(5, members[SPLIT_LOADS][0]):
            load_chunk(c)
        for g in range(SPLIT_LOADS, GROUPS_AHEAD):
            load_group(g)


        identity = const.tile([P, P], F32)
        make_identity(nc, identity[:])
        counts = const.tile([P, 1 + HALO, P], BF16)
        nc.gpsimd.memset(counts[:], float(TAPS))
        for t in range(HALO):
            nc.gpsimd.memset(counts[:, 1 + t, 0:1], float(t + 1))
        warm_col = const.tile([P, 1], F32)
        nc.vector.memset(warm_col[:], 0.0)
        nc.scalar.activation(out=warm_col[:], in_=warm_col[:], func=mybir.ActivationFunctionType.Tanh)
        nc.vector.memset(halo_codes[:].bitcast(I32), 0)
        nc.vector.memset(halo_scales[:].bitcast(I32), 0)
        nc.vector.memset(x_scales[:, SECTIONS - HALO : SECTIONS, :].bitcast(I32), 0)

        sorted_tiles = {}
        for c in range(SORT_AHEAD):
            sorted_tiles[c] = sort_chunk(c)

        bias = const.tile([P, 1 + HALO, C], F32)
        assert outputs[1] == list(range(HALO))

        def make_bias():
            bias_bank = acc_pool.tile([P, ACC_SECTIONS, C], F32, name="acc")
            for v in range(1 + HALO):
                nc.tensor.matmul(out=bias_bank[:, v, :], lhsT=counts[:, v, :], rhs=b1_row[:], start=True, stop=True)
            nc.scalar.copy(out=bias[:], in_=bias_bank[:, 0 : 1 + HALO, :])

        grouped_tiles = {}
        acc_banks = {}
        for i in range(n_chunks + 3):
            if i < n_chunks and i == members[group_of[i]][0] and group_of[i] + GROUPS_AHEAD < n_groups:
                load_group(group_of[i] + GROUPS_AHEAD)
            if 0 <= i - 3 and acc_banks[i - 3]:
                add_bias(i - 3, acc_banks[i - 3])
            if 0 <= i - 1 < n_chunks:
                quantise_chunk(i - 1, grouped_tiles[i - 1])
                if i - 1 == 0:
                    make_halo()
            if SORT_AHEAD <= i + SORT_AHEAD < n_chunks:
                sorted_tiles[i + SORT_AHEAD] = sort_chunk(i + SORT_AHEAD)
            if i < n_chunks:
                grouped_tiles[i] = transpose_chunk(i, sorted_tiles[i])
            if i == 3:
                make_bias()
            if 0 <= i - 2 < n_chunks:
                acc_banks[i - 2] = multiply_chunk(i - 2)
            if 0 <= i - 3 and acc_banks[i - 3]:
                tanh_and_store(i - 3)
